import numpy as np
import ml_dtypes


def mxq(x, axis, fmt="e4m3"):
    dtype, down = {"e4m3": (ml_dtypes.float8_e4m3fn, 7), "e5m2": (ml_dtypes.float8_e5m2, 14)}[fmt]
    v = np.moveaxis(np.asarray(x, np.float32).astype(ml_dtypes.bfloat16).astype(np.float64), axis, -1)
    blocks = v.reshape(v.shape[:-1] + (-1, 32))
    amax = np.abs(blocks).max(-1, keepdims=True)
    byte = np.maximum(np.where(amax > 0, np.frexp(amax)[1] - 1 + 127, 0) - down, 1)
    scale = np.exp2(byte - 127.0)
    codes = (blocks / scale).astype(np.float32).astype(dtype).astype(np.float64)
    return np.moveaxis((codes * scale).reshape(v.shape), -1, axis)


WIDE = False


def mx_kscale(k):
    if not WIDE:
        return np.ones(k)
    levels = np.array([20, -20, 10, -10, 0])
    a = np.random.permutation(np.resize(levels, k // 512 * 4)).reshape(k // 512, 4)
    idx = np.arange(k)
    return np.exp2(a[idx // 512, idx % 128 // 32])


BF16 = ml_dtypes.bfloat16


def bf(x):
    return np.asarray(x, np.float32).astype(BF16)


def f64(x):
    return np.asarray(x).astype(np.float64)


B, A, C, P = 256, 1, 512, 16384
N = A * A + 1


def scramble(y):
    return y.transpose(0, 2, 1).reshape(B, N, C)


def unscramble(z):
    return z.reshape(B, C, N).transpose(0, 2, 1)


def setup_inputs():
    u = mx_kscale(P)
    z = np.random.standard_normal((B, N, C)) * 1.6 / np.sqrt(N)
    w = np.random.standard_normal((P, C)) * 2.0 / np.sqrt(C) / u[:, None]
    b = np.random.standard_normal(P) * 0.1
    g = np.random.standard_normal((B, N, P)) * np.exp2(np.random.randint(-12, 1, (B, N, 1))) * 4.0 * u
    return {"y_attn": bf(np.ascontiguousarray(unscramble(z))),
            "w_proj": bf(w),
            "b_proj": bf(b),
            "grad_out": bf(g)}


def reference(y_attn, w_proj, b_proj, grad_out):
    gz = mxq(f64(grad_out), 2, "e5m2") @ mxq(f64(w_proj), 0, "e4m3")
    return np.ascontiguousarray(unscramble(gz))

@@ -1,0 +1,173 @@
+from contextlib import ExitStack
+
+import concourse.mybir as mybir
+from concourse.masks import make_identity
+
+BF16 = mybir.dt.bfloat16
+F32 = mybir.dt.float32
+U32 = mybir.dt.uint32
+U8 = mybir.dt.uint8
+E4M3_X4 = mybir.dt.float8_e4m3fn_x4
+E5M2_X4 = mybir.dt.float8_e5m2_x4
+
+P = 128
+PACK = 4
+K_PASS = P * PACK
+K = 16384
+ROWS = 512
+COLS = 512
+N_PASS = K // K_PASS
+ROW_TILES = ROWS // P
+WORDS_PASS = K_PASS // 2
+
+FLOPS = 2 * ROWS * COLS * K
+BYTES = 2 * ROWS * K + 2 * K * COLS + 4 * ROWS * COLS
+
+G_LOAD_PASSES = 4
+G_LOAD_K = G_LOAD_PASSES * K_PASS
+G_RAW_BUFS = 3
+W_RAW_BUFS = 8
+
+TRANSPOSE_LEAD = 3
+COPY_LEAD = 2
+G_QUANT_LEAD = 1
+W_LOAD_LEAD = W_RAW_BUFS - 1
+G_LOAD_LEAD = G_RAW_BUFS * G_LOAD_PASSES - 1
+
+VECTOR_COLS = 320
+RUN = 4
+
+
+def tile_attention_pa_k_kernel(tc, y_attn, w_proj, b_proj, grad_out, out):
+    nc = tc.nc
+
+    g_rows = grad_out.rearrange("(p b) i k -> p (b i) k", b=2)
+    w_rows = w_proj.rearrange("(h p e) c -> p h (e c)", p=P, e=2)
+    out_rows = out.rearrange("(p b) n c -> p b (n c)", b=2)
+
+    with ExitStack() as ctx:
+        const = ctx.enter_context(tc.tile_pool(name="const", bufs=1))
+        g_raw_pool = ctx.enter_context(tc.tile_pool(name="g_raw_pool", bufs=G_RAW_BUFS))
+        w_raw_pool = ctx.enter_context(tc.tile_pool(name="w_raw_pool", bufs=W_RAW_BUFS))
+        grouped_pool = ctx.enter_context(tc.tile_pool(name="grouped_pool", bufs=3))
+        quantised_pool = ctx.enter_context(tc.tile_pool(name="quantised_pool", bufs=4))
+        acc_pool = ctx.enter_context(tc.psum_pool(name="acc_pool", bufs=1))
+        bank_pool = ctx.enter_context(tc.psum_pool(name="bank_pool", bufs=4))
+
+        ident = const.tile([P, P], F32, name="ident")
+        make_identity(nc, ident[:])
+
+        acc = [acc_pool.tile([P, COLS], F32, name="acc%d" % m) for m in range(ROW_TILES)]
+
+        g_raw = {}
+        w_raw = {}
+        g_banks = {}
+        g_grouped = {}
+        g_quantised = {}
+        w_quantised = {}
+
+        def load_g(chunk):
+            raw = g_raw_pool.tile([P, ROW_TILES * G_LOAD_K], BF16, name="g_raw")
+            nc.sync.dma_start(
+                out=raw[:].rearrange("p (m k) -> p m k", m=ROW_TILES),
+                in_=g_rows[:, :, chunk * G_LOAD_K : (chunk + 1) * G_LOAD_K],
+            )
+            g_raw[chunk] = raw
+
+        def load_w(x):
+            raw = w_raw_pool.tile([P, PACK * COLS], BF16, name="w_raw")
+            nc.sync.dma_start(
+                out=raw[:].rearrange("p (u ec) -> p u ec", u=2),
+                in_=w_rows[:, 2 * x : 2 * x + 2, :],
+            )
+            w_raw[x] = raw
+
+        def transpose_g(x):
+            chunk, local = divmod(x, G_LOAD_PASSES)
+            words = g_raw[chunk][:].bitcast(F32).rearrange("p (m w) -> p m w", m=ROW_TILES)
+            g_banks[x] = []
+            for pair in range(ROW_TILES // 2):
+                bank = bank_pool.tile([P, 2, 2, P], F32, name="bank")
+                for mm in range(2):
+                    for u in range(2):
+                        first = local * WORDS_PASS + u * P
+                        nc.tensor.transpose(
+                            bank[:, mm, u, :], words[:, 2 * pair + mm, first : first + P], ident[:]
+                        )
+                g_banks[x].append(bank)
+
+        def copy_g(x):
+            grouped = grouped_pool.tile([P, ROWS * PACK], BF16, name="g_grouped", align_bytes=64)
+            words = grouped[:].bitcast(F32).rearrange("p (m r u) -> p m r u", m=ROW_TILES, u=2)
+            for pair in range(ROW_TILES // 2):
+                nc.scalar.copy(
+                    out=words[:, 2 * pair : 2 * pair + 2],
+                    in_=g_banks[x][pair][:].rearrange("p m u r -> p m r u"),
+                )
+            g_grouped[x] = grouped
+
+        def quantise(grouped, width, fp8_x4, name):
+            codes = quantised_pool.tile([P, width], U32, name=name + "_codes", align_bytes=64)
+            scales = quantised_pool.tile([P, width], U8, name=name + "_scales", align_bytes=64)
+            nc.vector.quantize_mx(out=codes[:].bitcast(fp8_x4), scales=scales[:], in_=grouped[:])
+            return codes, scales
+
+        def regroup_w(x):
+            grouped = grouped_pool.tile([P, COLS * PACK], BF16, name="w_grouped", align_bytes=64)
+            dst = grouped[:].rearrange("p (c i t) -> p c t i", i=RUN, t=PACK)
+            src = w_raw[x][:].rearrange("p (t c i) -> p c t i", t=PACK, i=RUN)
+            split = VECTOR_COLS // RUN
+            nc.vector.tensor_copy(out=dst[:, :split], in_=src[:, :split])
+            nc.scalar.copy(out=dst[:, split:], in_=src[:, split:])
+            return grouped
+
+        def multiply(x):
+            g_codes, g_scales = g_quantised[x]
+            w_codes, w_scales = w_quantised[x]
+            for m in range(ROW_TILES):
+                tile_rows = slice(m * P, (m + 1) * P)
+                nc.tensor.matmul_mx(
+                    out=acc[m][:],
+                    lhsT=g_codes[:, tile_rows].bitcast(E5M2_X4),
+                    lhsT_scale=g_scales[:, tile_rows],
+                    rhs=w_codes[:].bitcast(E4M3_X4),
+                    rhs_scale=w_scales[:],
+                    start=(x == 0),
+                    stop=(x == N_PASS - 1),
+                )
+
+        def is_pass(x):
+            return 0 <= x < N_PASS
+
+        with tc.manual_schedule():
+            for r in range(-G_LOAD_LEAD, N_PASS + 1):
+                if is_pass(r + G_LOAD_LEAD) and (r + G_LOAD_LEAD) % G_LOAD_PASSES == 0:
+                    load_g((r + G_LOAD_LEAD) // G_LOAD_PASSES)
+                if is_pass(r + W_LOAD_LEAD):
+                    load_w(r + W_LOAD_LEAD)
+                if is_pass(r + TRANSPOSE_LEAD):
+                    transpose_g(r + TRANSPOSE_LEAD)
+                if is_pass(r + COPY_LEAD):
+                    copy_g(r + COPY_LEAD)
+                if is_pass(r):
+                    w_grouped = regroup_w(r)
+                if is_pass(r + G_QUANT_LEAD):
+                    g_quantised[r + G_QUANT_LEAD] = quantise(
+                        g_grouped[r + G_QUANT_LEAD], ROWS, E5M2_X4, "g"
+                    )
+                if is_pass(r):
+                    w_quantised[r] = quantise(w_grouped, COLS, E4M3_X4, "w")
+                if is_pass(r - 1):
+                    multiply(r - 1)
+
+            result = const.tile([P, 2, 2, 2, COLS // 2], F32, name="result")
+            for m in range(ROW_TILES):
+                h, i = divmod(m, 2)
+                sums = acc[m][:].rearrange("p (j n) -> p n j", n=2)
+                if i == 0:
+                    nc.scalar.copy(out=result[:, h, :, i, :], in_=sums)
+                else:
+                    nc.vector.tensor_copy(out=result[:, h, :, i, :], in_=sums)
+                    nc.sync.dma_start(
+                        out=out_rows[:, h, :], in_=result[:, h].rearrange("p n i j -> p (n i j)")
+                    )

@@ -28,11 +28,12 @@ G_LOAD_K = G_LOAD_PASSES * K_PASS
 G_RAW_BUFS = 3
 W_RAW_BUFS = 8
 
-TRANSPOSE_LEAD = 3
-COPY_LEAD = 2
-G_QUANT_LEAD = 1
-W_LOAD_LEAD = W_RAW_BUFS - 1
-G_LOAD_LEAD = G_RAW_BUFS * G_LOAD_PASSES - 1
+ROUND = 2
+COPY_LEAD = 4
+G_QUANT_LEAD = 2
+W_LEAD = 1
+W_LOAD_LEAD = W_RAW_BUFS
+G_LOAD_LEAD = G_RAW_BUFS * G_LOAD_PASSES
 
 VECTOR_COLS = 320
 RUN = 4
@@ -49,8 +50,8 @@ def tile_attention_pa_k_kernel(tc, y_attn, w_proj, b_proj, grad_out, out):
         const = ctx.enter_context(tc.tile_pool(name="const", bufs=1))
         g_raw_pool = ctx.enter_context(tc.tile_pool(name="g_raw_pool", bufs=G_RAW_BUFS))
         w_raw_pool = ctx.enter_context(tc.tile_pool(name="w_raw_pool", bufs=W_RAW_BUFS))
-        grouped_pool = ctx.enter_context(tc.tile_pool(name="grouped_pool", bufs=3))
-        quantised_pool = ctx.enter_context(tc.tile_pool(name="quantised_pool", bufs=4))
+        grouped_pool = ctx.enter_context(tc.tile_pool(name="grouped_pool", bufs=4))
+        quantised_pool = ctx.enter_context(tc.tile_pool(name="quantised_pool", bufs=6))
         acc_pool = ctx.enter_context(tc.psum_pool(name="acc_pool", bufs=1))
         bank_pool = ctx.enter_context(tc.psum_pool(name="bank_pool", bufs=4))
 
@@ -140,25 +141,28 @@ def tile_attention_pa_k_kernel(tc, y_attn, w_proj, b_proj, grad_out, out):
             return 0 <= x < N_PASS
 
         with tc.manual_schedule():
-            for r in range(-G_LOAD_LEAD, N_PASS + 1):
-                if is_pass(r + G_LOAD_LEAD) and (r + G_LOAD_LEAD) % G_LOAD_PASSES == 0:
-                    load_g((r + G_LOAD_LEAD) // G_LOAD_PASSES)
-                if is_pass(r + W_LOAD_LEAD):
-                    load_w(r + W_LOAD_LEAD)
-                if is_pass(r + TRANSPOSE_LEAD):
-                    transpose_g(r + TRANSPOSE_LEAD)
-                if is_pass(r + COPY_LEAD):
-                    copy_g(r + COPY_LEAD)
-                if is_pass(r):
-                    w_grouped = regroup_w(r)
-                if is_pass(r + G_QUANT_LEAD):
-                    g_quantised[r + G_QUANT_LEAD] = quantise(
-                        g_grouped[r + G_QUANT_LEAD], ROWS, E5M2_X4, "g"
-                    )
-                if is_pass(r):
-                    w_quantised[r] = quantise(w_grouped, COLS, E4M3_X4, "w")
-                if is_pass(r - 1):
-                    multiply(r - 1)
+            for r in range(-G_LOAD_LEAD, N_PASS + ROUND, ROUND):
+                for x in range(r, r + ROUND):
+                    if is_pass(x + COPY_LEAD):
+                        transpose_g(x + COPY_LEAD)
+                for x in range(r, r + ROUND):
+                    if is_pass(x + G_LOAD_LEAD) and (x + G_LOAD_LEAD) % G_LOAD_PASSES == 0:
+                        load_g((x + G_LOAD_LEAD) // G_LOAD_PASSES)
+                    if is_pass(x + W_LOAD_LEAD):
+                        load_w(x + W_LOAD_LEAD)
+                    if is_pass(x + COPY_LEAD):
+                        copy_g(x + COPY_LEAD)
+                    if is_pass(x + W_LEAD):
+                        w_grouped = regroup_w(x + W_LEAD)
+                    if is_pass(x + G_QUANT_LEAD):
+                        g_quantised[x + G_QUANT_LEAD] = quantise(
+                            g_grouped[x + G_QUANT_LEAD], ROWS, E5M2_X4, "g"
+                        )
+                    if is_pass(x + W_LEAD):
+                        w_quantised[x + W_LEAD] = quantise(w_grouped, COLS, E4M3_X4, "w")
+                for x in range(r - 1, r - 1 + ROUND):
+                    if is_pass(x):
+                        multiply(x)
 
             result = const.tile([P, 2, 2, 2, COLS // 2], F32, name="result")
             for m in range(ROW_TILES):

@@ -23,17 +23,16 @@ WORDS_PASS = K_PASS // 2
 FLOPS = 2 * ROWS * COLS * K
 BYTES = 2 * ROWS * K + 2 * K * COLS + 4 * ROWS * COLS
 
-G_LOAD_PASSES = 4
-G_LOAD_K = G_LOAD_PASSES * K_PASS
-G_RAW_BUFS = 3
-W_RAW_BUFS = 8
+CHUNK = ROW_TILES
+CHUNK_K = CHUNK * K_PASS
+N_STEP = N_PASS
+RAW_BUFS = 8
 
-ROUND = 2
-COPY_LEAD = 4
-G_QUANT_LEAD = 2
-W_LEAD = 1
-W_LOAD_LEAD = W_RAW_BUFS
-G_LOAD_LEAD = G_RAW_BUFS * G_LOAD_PASSES
+TRANSPOSE_LEAD = 3
+COPY_LEAD = 2
+G_QUANT_LEAD = 1
+W_LOAD_LEAD = RAW_BUFS - 1
+G_LOAD_LEAD = W_LOAD_LEAD + 2
 
 VECTOR_COLS = 320
 RUN = 4
@@ -48,10 +47,9 @@ def tile_attention_pa_k_kernel(tc, y_attn, w_proj, b_proj, grad_out, out):
 
     with ExitStack() as ctx:
         const = ctx.enter_context(tc.tile_pool(name="const", bufs=1))
-        g_raw_pool = ctx.enter_context(tc.tile_pool(name="g_raw_pool", bufs=G_RAW_BUFS))
-        w_raw_pool = ctx.enter_context(tc.tile_pool(name="w_raw_pool", bufs=W_RAW_BUFS))
-        grouped_pool = ctx.enter_context(tc.tile_pool(name="grouped_pool", bufs=4))
-        quantised_pool = ctx.enter_context(tc.tile_pool(name="quantised_pool", bufs=6))
+        raw_pool = ctx.enter_context(tc.tile_pool(name="raw_pool", bufs=RAW_BUFS))
+        grouped_pool = ctx.enter_context(tc.tile_pool(name="grouped_pool", bufs=3))
+        quantised_pool = ctx.enter_context(tc.tile_pool(name="quantised_pool", bufs=2 * CHUNK))
         acc_pool = ctx.enter_context(tc.psum_pool(name="acc_pool", bufs=1))
         bank_pool = ctx.enter_context(tc.psum_pool(name="bank_pool", bufs=4))
 
@@ -67,45 +65,40 @@ def tile_attention_pa_k_kernel(tc, y_attn, w_proj, b_proj, grad_out, out):
         g_quantised = {}
         w_quantised = {}
 
-        def load_g(chunk):
-            raw = g_raw_pool.tile([P, ROW_TILES * G_LOAD_K], BF16, name="g_raw")
-            nc.sync.dma_start(
-                out=raw[:].rearrange("p (m k) -> p m k", m=ROW_TILES),
-                in_=g_rows[:, :, chunk * G_LOAD_K : (chunk + 1) * G_LOAD_K],
-            )
-            g_raw[chunk] = raw
+        def load_g(s):
+            j, i = divmod(s, CHUNK)
+            raw = raw_pool.tile([P, CHUNK_K], BF16, name="g_raw")
+            nc.sync.dma_start(out=raw[:], in_=g_rows[:, i, j * CHUNK_K : (j + 1) * CHUNK_K])
+            g_raw[s] = raw
 
-        def load_w(x):
-            raw = w_raw_pool.tile([P, PACK * COLS], BF16, name="w_raw")
+        def load_w(s):
+            raw = raw_pool.tile([P, PACK * COLS], BF16, name="w_raw")
             nc.sync.dma_start(
                 out=raw[:].rearrange("p (u ec) -> p u ec", u=2),
-                in_=w_rows[:, 2 * x : 2 * x + 2, :],
+                in_=w_rows[:, 2 * s : 2 * s + 2, :],
             )
-            w_raw[x] = raw
+            w_raw[s] = raw
 
-        def transpose_g(x):
-            chunk, local = divmod(x, G_LOAD_PASSES)
-            words = g_raw[chunk][:].bitcast(F32).rearrange("p (m w) -> p m w", m=ROW_TILES)
-            g_banks[x] = []
-            for pair in range(ROW_TILES // 2):
+        def transpose_g(s):
+            words = g_raw[s][:].bitcast(F32)
+            g_banks[s] = []
+            for pair in range(CHUNK // 2):
                 bank = bank_pool.tile([P, 2, 2, P], F32, name="bank")
-                for mm in range(2):
+                for aa in range(2):
                     for u in range(2):
-                        first = local * WORDS_PASS + u * P
-                        nc.tensor.transpose(
-                            bank[:, mm, u, :], words[:, 2 * pair + mm, first : first + P], ident[:]
-                        )
-                g_banks[x].append(bank)
+                        first = (2 * pair + aa) * WORDS_PASS + u * P
+                        nc.tensor.transpose(bank[:, aa, u, :], words[:, first : first + P], ident[:])
+                g_banks[s].append(bank)
 
-        def copy_g(x):
-            grouped = grouped_pool.tile([P, ROWS * PACK], BF16, name="g_grouped", align_bytes=64)
-            words = grouped[:].bitcast(F32).rearrange("p (m r u) -> p m r u", m=ROW_TILES, u=2)
-            for pair in range(ROW_TILES // 2):
+        def copy_g(s):
+            grouped = grouped_pool.tile([P, CHUNK * P * PACK], BF16, name="g_grouped", align_bytes=64)
+            words = grouped[:].bitcast(F32).rearrange("p (a r u) -> p a r u", a=CHUNK, u=2)
+            for pair in range(CHUNK // 2):
                 nc.scalar.copy(
                     out=words[:, 2 * pair : 2 * pair + 2],
-                    in_=g_banks[x][pair][:].rearrange("p m u r -> p m r u"),
+                    in_=g_banks[s][pair][:].rearrange("p a u r -> p a r u"),
                 )
-            g_grouped[x] = grouped
+            g_grouped[s] = grouped
 
         def quantise(grouped, width, fp8_x4, name):
             codes = quantised_pool.tile([P, width], U32, name=name + "_codes", align_bytes=64)
@@ -113,56 +106,60 @@ def tile_attention_pa_k_kernel(tc, y_attn, w_proj, b_proj, grad_out, out):
             nc.vector.quantize_mx(out=codes[:].bitcast(fp8_x4), scales=scales[:], in_=grouped[:])
             return codes, scales
 
-        def regroup_w(x):
+        def regroup_w(s):
             grouped = grouped_pool.tile([P, COLS * PACK], BF16, name="w_grouped", align_bytes=64)
             dst = grouped[:].rearrange("p (c i t) -> p c t i", i=RUN, t=PACK)
-            src = w_raw[x][:].rearrange("p (t c i) -> p c t i", t=PACK, i=RUN)
+            src = w_raw[s][:].rearrange("p (t c i) -> p c t i", t=PACK, i=RUN)
             split = VECTOR_COLS // RUN
             nc.vector.tensor_copy(out=dst[:, :split], in_=src[:, :split])
             nc.scalar.copy(out=dst[:, split:], in_=src[:, split:])
             return grouped
 
-        def multiply(x):
-            g_codes, g_scales = g_quantised[x]
+        def multiply(m, x):
+            j, a = divmod(x, CHUNK)
+            g_codes, g_scales = g_quantised[j * CHUNK + m]
             w_codes, w_scales = w_quantised[x]
-            for m in range(ROW_TILES):
-                tile_rows = slice(m * P, (m + 1) * P)
-                nc.tensor.matmul_mx(
-                    out=acc[m][:],
-                    lhsT=g_codes[:, tile_rows].bitcast(E5M2_X4),
-                    lhsT_scale=g_scales[:, tile_rows],
-                    rhs=w_codes[:].bitcast(E4M3_X4),
-                    rhs_scale=w_scales[:],
-                    start=(x == 0),
-                    stop=(x == N_PASS - 1),
-                )
+            pass_rows = slice(a * P, (a + 1) * P)
+            nc.tensor.matmul_mx(
+                out=acc[m][:],
+                lhsT=g_codes[:, pass_rows].bitcast(E5M2_X4),
+                lhsT_scale=g_scales[:, pass_rows],
+                rhs=w_codes[:].bitcast(E4M3_X4),
+                rhs_scale=w_scales[:],
+                start=(x == 0),
+                stop=(x == N_PASS - 1),
+            )
 
-        def is_pass(x):
-            return 0 <= x < N_PASS
+        def multiply_new(s):
+            j, i = divmod(s, CHUNK)
+            for a in range(i):
+                multiply(i, j * CHUNK + a)
+            for m in range(i + 1):
+                multiply(m, s)
+
+        def is_step(s):
+            return 0 <= s < N_STEP
 
         with tc.manual_schedule():
-            for r in range(-G_LOAD_LEAD, N_PASS + ROUND, ROUND):
-                for x in range(r, r + ROUND):
-                    if is_pass(x + COPY_LEAD):
-                        transpose_g(x + COPY_LEAD)
-                for x in range(r, r + ROUND):
-                    if is_pass(x + G_LOAD_LEAD) and (x + G_LOAD_LEAD) % G_LOAD_PASSES == 0:
-                        load_g((x + G_LOAD_LEAD) // G_LOAD_PASSES)
-                    if is_pass(x + W_LOAD_LEAD):
-                        load_w(x + W_LOAD_LEAD)
-                    if is_pass(x + COPY_LEAD):
-                        copy_g(x + COPY_LEAD)
-                    if is_pass(x + W_LEAD):
-                        w_grouped = regroup_w(x + W_LEAD)
-                    if is_pass(x + G_QUANT_LEAD):
-                        g_quantised[x + G_QUANT_LEAD] = quantise(
-                            g_grouped[x + G_QUANT_LEAD], ROWS, E5M2_X4, "g"
-                        )
-                    if is_pass(x + W_LEAD):
-                        w_quantised[x + W_LEAD] = quantise(w_grouped, COLS, E4M3_X4, "w")
-                for x in range(r - 1, r - 1 + ROUND):
-                    if is_pass(x):
-                        multiply(x)
+            for r in range(-G_LOAD_LEAD, N_STEP + 1):
+                if is_step(r + G_LOAD_LEAD):
+                    load_g(r + G_LOAD_LEAD)
+                if is_step(r + W_LOAD_LEAD):
+                    load_w(r + W_LOAD_LEAD)
+                if is_step(r + TRANSPOSE_LEAD):
+                    transpose_g(r + TRANSPOSE_LEAD)
+                if is_step(r + COPY_LEAD):
+                    copy_g(r + COPY_LEAD)
+                if is_step(r):
+                    w_grouped = regroup_w(r)
+                if is_step(r + G_QUANT_LEAD):
+                    g_quantised[r + G_QUANT_LEAD] = quantise(
+                        g_grouped[r + G_QUANT_LEAD], CHUNK * P, E5M2_X4, "g"
+                    )
+                if is_step(r):
+                    w_quantised[r] = quantise(w_grouped, COLS, E4M3_X4, "w")
+                if is_step(r - 1):
+                    multiply_new(r - 1)
 
             result = const.tile([P, 2, 2, 2, COLS // 2], F32, name="result")
             for m in range(ROW_TILES):

@@ -23,19 +23,39 @@ WORDS_PASS = K_PASS // 2
 FLOPS = 2 * ROWS * COLS * K
 BYTES = 2 * ROWS * K + 2 * K * COLS + 4 * ROWS * COLS
 
-CHUNK = ROW_TILES
-CHUNK_K = CHUNK * K_PASS
-N_STEP = N_PASS
+PIECE_PASSES = 4
 RAW_BUFS = 8
 
-TRANSPOSE_LEAD = 3
-COPY_LEAD = 2
-G_QUANT_LEAD = 1
-W_LOAD_LEAD = RAW_BUFS - 1
-G_LOAD_LEAD = W_LOAD_LEAD + 2
+HALVED_ROW_TILES = (2, 3)
 
 VECTOR_COLS = 320
 RUN = 4
+
+LOAD_LEAD = 2 * RAW_BUFS - 1
+COPY_LAG = 1
+G_QUANT_LAG = 3
+W_QUANT_LAG = 1
+PRODUCT_LAG = 2
+OUT_LAG = 2
+FLUSH = 12
+
+
+def stream():
+    pieces = []
+    for x0 in range(0, N_PASS, PIECE_PASSES):
+        for m in range(ROW_TILES):
+            if x0 == N_PASS - PIECE_PASSES and m in HALVED_ROW_TILES:
+                half = PIECE_PASSES // 2
+                pieces.append(("g", m, x0, half))
+                pieces.append(("g", m, x0 + half, half))
+            else:
+                pieces.append(("g", m, x0, PIECE_PASSES))
+    items = [("w", 0)]
+    for x in range(1, N_PASS):
+        items.append(("w", x))
+        items.append(pieces[x - 1])
+    items.extend(pieces[N_PASS - 1 :])
+    return items
 
 
 def tile_attention_pa_k_kernel(tc, y_attn, w_proj, b_proj, grad_out, out):
@@ -43,132 +63,143 @@ def tile_attention_pa_k_kernel(tc, y_attn, w_proj, b_proj, grad_out, out):
 
     g_rows = grad_out.rearrange("(p b) i k -> p (b i) k", b=2)
     w_rows = w_proj.rearrange("(h p e) c -> p h (e c)", p=P, e=2)
-    out_rows = out.rearrange("(p b) n c -> p b (n c)", b=2)
+    out_rows = out.rearrange("(p b) n (i j) -> p b n i j", b=2, i=2)
+
+    items = stream()
+    n_items = len(items)
 
     with ExitStack() as ctx:
         const = ctx.enter_context(tc.tile_pool(name="const", bufs=1))
         raw_pool = ctx.enter_context(tc.tile_pool(name="raw_pool", bufs=RAW_BUFS))
         grouped_pool = ctx.enter_context(tc.tile_pool(name="grouped_pool", bufs=3))
-        quantised_pool = ctx.enter_context(tc.tile_pool(name="quantised_pool", bufs=2 * CHUNK))
+        g_quantised_pool = ctx.enter_context(tc.tile_pool(name="g_quantised_pool", bufs=8))
+        w_quantised_pool = ctx.enter_context(tc.tile_pool(name="w_quantised_pool", bufs=12))
         acc_pool = ctx.enter_context(tc.psum_pool(name="acc_pool", bufs=1))
         bank_pool = ctx.enter_context(tc.psum_pool(name="bank_pool", bufs=4))
 
         ident = const.tile([P, P], F32, name="ident")
         make_identity(nc, ident[:])
+        result = const.tile([P, 2, 2, 2, COLS // 2], F32, name="result")
 
         acc = [acc_pool.tile([P, COLS], F32, name="acc%d" % m) for m in range(ROW_TILES)]
 
-        g_raw = {}
-        w_raw = {}
-        g_banks = {}
-        g_grouped = {}
+        raw = {}
+        banks = {}
+        grouped = {}
         g_quantised = {}
         w_quantised = {}
+        enabled = {}
+        finished = {}
+        done = [0] * ROW_TILES
 
-        def load_g(s):
-            j, i = divmod(s, CHUNK)
-            raw = raw_pool.tile([P, CHUNK_K], BF16, name="g_raw")
-            nc.sync.dma_start(out=raw[:], in_=g_rows[:, i, j * CHUNK_K : (j + 1) * CHUNK_K])
-            g_raw[s] = raw
+        def load(n):
+            item = items[n]
+            if item[0] == "w":
+                x = item[1]
+                tile = raw_pool.tile([P, PACK * COLS], BF16, name="w_raw")
+                nc.sync.dma_start(
+                    out=tile[:].rearrange("p (u ec) -> p u ec", u=2),
+                    in_=w_rows[:, 2 * x : 2 * x + 2, :],
+                )
+            else:
+                m, x0, passes = item[1:]
+                tile = raw_pool.tile([P, passes * K_PASS], BF16, name="g_raw")
+                nc.sync.dma_start(out=tile[:], in_=g_rows[:, m, x0 * K_PASS : (x0 + passes) * K_PASS])
+            raw[n] = tile
 
-        def load_w(s):
-            raw = raw_pool.tile([P, PACK * COLS], BF16, name="w_raw")
-            nc.sync.dma_start(
-                out=raw[:].rearrange("p (u ec) -> p u ec", u=2),
-                in_=w_rows[:, 2 * s : 2 * s + 2, :],
-            )
-            w_raw[s] = raw
-
-        def transpose_g(s):
-            words = g_raw[s][:].bitcast(F32)
-            g_banks[s] = []
-            for pair in range(CHUNK // 2):
+        def transpose_g(n):
+            passes = items[n][3]
+            words = raw[n][:].bitcast(F32)
+            banks[n] = []
+            for pair in range(passes // 2):
                 bank = bank_pool.tile([P, 2, 2, P], F32, name="bank")
                 for aa in range(2):
                     for u in range(2):
                         first = (2 * pair + aa) * WORDS_PASS + u * P
                         nc.tensor.transpose(bank[:, aa, u, :], words[:, first : first + P], ident[:])
-                g_banks[s].append(bank)
+                banks[n].append(bank)
 
-        def copy_g(s):
-            grouped = grouped_pool.tile([P, CHUNK * P * PACK], BF16, name="g_grouped", align_bytes=64)
-            words = grouped[:].bitcast(F32).rearrange("p (a r u) -> p a r u", a=CHUNK, u=2)
-            for pair in range(CHUNK // 2):
+        def copy_g(n):
+            passes = items[n][3]
+            tile = grouped_pool.tile([P, passes * P * PACK], BF16, name="g_grouped", align_bytes=64)
+            words = tile[:].bitcast(F32).rearrange("p (a r u) -> p a r u", a=passes, u=2)
+            for pair in range(passes // 2):
                 nc.scalar.copy(
                     out=words[:, 2 * pair : 2 * pair + 2],
-                    in_=g_banks[s][pair][:].rearrange("p a u r -> p a r u"),
+                    in_=banks[n][pair][:].rearrange("p a u r -> p a r u"),
                 )
-            g_grouped[s] = grouped
+            grouped[n] = tile
 
-        def quantise(grouped, width, fp8_x4, name):
-            codes = quantised_pool.tile([P, width], U32, name=name + "_codes", align_bytes=64)
-            scales = quantised_pool.tile([P, width], U8, name=name + "_scales", align_bytes=64)
-            nc.vector.quantize_mx(out=codes[:].bitcast(fp8_x4), scales=scales[:], in_=grouped[:])
-            return codes, scales
-
-        def regroup_w(s):
-            grouped = grouped_pool.tile([P, COLS * PACK], BF16, name="w_grouped", align_bytes=64)
-            dst = grouped[:].rearrange("p (c i t) -> p c t i", i=RUN, t=PACK)
-            src = w_raw[s][:].rearrange("p (t c i) -> p c t i", t=PACK, i=RUN)
+        def regroup_w(n):
+            tile = grouped_pool.tile([P, COLS * PACK], BF16, name="w_grouped", align_bytes=64)
+            dst = tile[:].rearrange("p (c i t) -> p c t i", i=RUN, t=PACK)
+            src = raw[n][:].rearrange("p (t c i) -> p c t i", t=PACK, i=RUN)
             split = VECTOR_COLS // RUN
             nc.vector.tensor_copy(out=dst[:, :split], in_=src[:, :split])
             nc.scalar.copy(out=dst[:, split:], in_=src[:, split:])
-            return grouped
+            grouped[n] = tile
+
+        def quantise(pool, n, width, fp8_x4, name):
+            codes = pool.tile([P, width], U32, name=name + "_codes", align_bytes=64)
+            scales = pool.tile([P, width], U8, name=name + "_scales", align_bytes=64)
+            nc.vector.quantize_mx(out=codes[:].bitcast(fp8_x4), scales=scales[:], in_=grouped[n][:])
+            return codes, scales
 
         def multiply(m, x):
-            j, a = divmod(x, CHUNK)
-            g_codes, g_scales = g_quantised[j * CHUNK + m]
+            g_codes, g_scales, first = g_quantised[(m, x)]
             w_codes, w_scales = w_quantised[x]
-            pass_rows = slice(a * P, (a + 1) * P)
+            g_cols = slice(first, first + P)
             nc.tensor.matmul_mx(
                 out=acc[m][:],
-                lhsT=g_codes[:, pass_rows].bitcast(E5M2_X4),
-                lhsT_scale=g_scales[:, pass_rows],
+                lhsT=g_codes[:, g_cols].bitcast(E5M2_X4),
+                lhsT_scale=g_scales[:, g_cols],
                 rhs=w_codes[:].bitcast(E4M3_X4),
                 rhs_scale=w_scales[:],
-                start=(x == 0),
-                stop=(x == N_PASS - 1),
+                start=(done[m] == 0),
+                stop=(done[m] == N_PASS - 1),
             )
+            done[m] += 1
 
-        def multiply_new(s):
-            j, i = divmod(s, CHUNK)
-            for a in range(i):
-                multiply(i, j * CHUNK + a)
-            for m in range(i + 1):
-                multiply(m, s)
+        def store(m):
+            h, i = divmod(m, 2)
+            sums = acc[m][:].rearrange("p (j n) -> p n j", n=2)
+            if m < ROW_TILES - 1:
+                nc.scalar.copy(out=result[:, h, :, i, :], in_=sums)
+            else:
+                nc.vector.tensor_copy(out=result[:, h, :, i, :], in_=sums)
+            nc.sync.dma_start(out=out_rows[:, h, :, i, :], in_=result[:, h, :, i, :])
 
-        def is_step(s):
-            return 0 <= s < N_STEP
+        def kind(n):
+            return items[n][0] if 0 <= n < n_items else ""
 
         with tc.manual_schedule():
-            for r in range(-G_LOAD_LEAD, N_STEP + 1):
-                if is_step(r + G_LOAD_LEAD):
-                    load_g(r + G_LOAD_LEAD)
-                if is_step(r + W_LOAD_LEAD):
-                    load_w(r + W_LOAD_LEAD)
-                if is_step(r + TRANSPOSE_LEAD):
-                    transpose_g(r + TRANSPOSE_LEAD)
-                if is_step(r + COPY_LEAD):
-                    copy_g(r + COPY_LEAD)
-                if is_step(r):
-                    w_grouped = regroup_w(r)
-                if is_step(r + G_QUANT_LEAD):
-                    g_quantised[r + G_QUANT_LEAD] = quantise(
-                        g_grouped[r + G_QUANT_LEAD], CHUNK * P, E5M2_X4, "g"
-                    )
-                if is_step(r):
-                    w_quantised[r] = quantise(w_grouped, COLS, E4M3_X4, "w")
-                if is_step(r - 1):
-                    multiply_new(r - 1)
-
-            result = const.tile([P, 2, 2, 2, COLS // 2], F32, name="result")
-            for m in range(ROW_TILES):
-                h, i = divmod(m, 2)
-                sums = acc[m][:].rearrange("p (j n) -> p n j", n=2)
-                if i == 0:
-                    nc.scalar.copy(out=result[:, h, :, i, :], in_=sums)
-                else:
-                    nc.vector.tensor_copy(out=result[:, h, :, i, :], in_=sums)
-                    nc.sync.dma_start(
-                        out=out_rows[:, h, :], in_=result[:, h].rearrange("p n i j -> p (n i j)")
-                    )
+            for tick in range(-LOAD_LEAD, n_items + FLUSH):
+                if kind(tick + LOAD_LEAD):
+                    load(tick + LOAD_LEAD)
+                if kind(tick) == "g":
+                    transpose_g(tick)
+                if kind(tick - COPY_LAG) == "g":
+                    copy_g(tick - COPY_LAG)
+                if kind(tick) == "w":
+                    regroup_w(tick)
+                new = []
+                if kind(tick - G_QUANT_LAG) == "g":
+                    n = tick - G_QUANT_LAG
+                    m, x0, passes = items[n][1:]
+                    codes, scales = quantise(g_quantised_pool, n, passes * P, E5M2_X4, "g")
+                    for a in range(passes):
+                        g_quantised[(m, x0 + a)] = (codes, scales, a * P)
+                        if x0 + a in w_quantised:
+                            new.append((m, x0 + a))
+                if kind(tick - W_QUANT_LAG) == "w":
+                    n = tick - W_QUANT_LAG
+                    x = items[n][1]
+                    w_quantised[x] = quantise(w_quantised_pool, n, COLS, E4M3_X4, "w")
+                    new.extend([(m, x) for m in range(ROW_TILES) if (m, x) in g_quantised])
+                enabled[tick] = new
+                for m, x in enabled.get(tick - PRODUCT_LAG, []):
+                    multiply(m, x)
+                    if done[m] == N_PASS:
+                        finished[tick] = finished.get(tick, []) + [m]
+                for m in finished.get(tick - OUT_LAG, []):
+                    store(m)

@@ -26,16 +26,16 @@ BYTES = 2 * ROWS * K + 2 * K * COLS + 4 * ROWS * COLS
 PIECE_PASSES = 4
 RAW_BUFS = 8
 
-HALVED_ROW_TILES = (2, 3)
+HALVED_ROW_TILES = (3,)
 
 VECTOR_COLS = 320
 RUN = 4
 
 LOAD_LEAD = 2 * RAW_BUFS - 1
 COPY_LAG = 1
-G_QUANT_LAG = 3
+G_QUANT_LAG = 2
 W_QUANT_LAG = 1
-PRODUCT_LAG = 2
+PRODUCT_LAG = 1
 OUT_LAG = 2
 FLUSH = 12
 
@@ -176,8 +176,11 @@ def tile_attention_pa_k_kernel(tc, y_attn, w_proj, b_proj, grad_out, out):
             for tick in range(-LOAD_LEAD, n_items + FLUSH):
                 if kind(tick + LOAD_LEAD):
                     load(tick + LOAD_LEAD)
-                if kind(tick) == "g":
-                    transpose_g(tick)
+                if kind(tick) == "g" and kind(tick - 1) != "g":
+                    n = tick
+                    while kind(n) == "g":
+                        transpose_g(n)
+                        n += 1
                 if kind(tick - COPY_LAG) == "g":
                     copy_g(tick - COPY_LAG)
                 if kind(tick) == "w":

@@ -165,9 +165,11 @@ def tile_attention_pa_k_kernel(tc, y_attn, w_proj, b_proj, grad_out, out):
             sums = acc[m][:].rearrange("p (j n) -> p n j", n=2)
             if m < ROW_TILES - 1:
                 nc.scalar.copy(out=result[:, h, :, i, :], in_=sums)
+                nc.sync.dma_start(out=out_rows[:, h, :, i, :], in_=result[:, h, :, i, :])
             else:
-                nc.vector.tensor_copy(out=result[:, h, :, i, :], in_=sums)
-            nc.sync.dma_start(out=out_rows[:, h, :, i, :], in_=result[:, h, :, i, :])
+                for n in range(2):
+                    nc.vector.tensor_copy(out=result[:, h, n, i, :], in_=sums[:, n, :])
+                    nc.sync.dma_start(out=out_rows[:, h, n, i, :], in_=result[:, h, n, i, :])
 
         def kind(n):
             return items[n][0] if 0 <= n < n_items else ""

@@ -26,7 +26,7 @@ BYTES = 2 * ROWS * K + 2 * K * COLS + 4 * ROWS * COLS
 PIECE_PASSES = 4
 RAW_BUFS = 8
 
-HALVED_ROW_TILES = (3,)
+HALVED_ROW_TILES = (1, 2, 3)
 
 VECTOR_COLS = 320
 RUN = 4
@@ -51,10 +51,11 @@ def stream():
             else:
                 pieces.append(("g", m, x0, PIECE_PASSES))
     items = [("w", 0)]
-    for x in range(1, N_PASS):
+    for x in range(1, N_PASS - 2):
         items.append(("w", x))
         items.append(pieces[x - 1])
-    items.extend(pieces[N_PASS - 1 :])
+    items.extend([pieces[N_PASS - 3], ("w", N_PASS - 2), pieces[N_PASS - 2], pieces[N_PASS - 1], ("w", N_PASS - 1)])
+    items.extend(pieces[N_PASS:])
     return items
 
 

from contextlib import ExitStack

import concourse.mybir as mybir
from concourse.masks import make_identity

BF16 = mybir.dt.bfloat16
F32 = mybir.dt.float32
U32 = mybir.dt.uint32
U8 = mybir.dt.uint8
E4M3_X4 = mybir.dt.float8_e4m3fn_x4
E5M2_X4 = mybir.dt.float8_e5m2_x4

P = 128
PACK = 4
K_PASS = P * PACK
K = 16384
ROWS = 512
COLS = 512
N_PASS = K // K_PASS
ROW_TILES = ROWS // P
WORDS_PASS = K_PASS // 2

FLOPS = 2 * ROWS * COLS * K
BYTES = 2 * ROWS * K + 2 * K * COLS + 4 * ROWS * COLS

PIECE_PASSES = 4
RAW_BUFS = 8

HALVED_ROW_TILES = (1, 2, 3)

VECTOR_COLS = 320
RUN = 4

LOAD_LEAD = 2 * RAW_BUFS - 1
COPY_LAG = 1
G_QUANT_LAG = 2
W_QUANT_LAG = 1
PRODUCT_LAG = 1
OUT_LAG = 2
FLUSH = 12


def stream():
    pieces = []
    for x0 in range(0, N_PASS, PIECE_PASSES):
        for m in range(ROW_TILES):
            if x0 == N_PASS - PIECE_PASSES and m in HALVED_ROW_TILES:
                half = PIECE_PASSES // 2
                pieces.append(("g", m, x0, half))
                pieces.append(("g", m, x0 + half, half))
            else:
                pieces.append(("g", m, x0, PIECE_PASSES))
    items = [("w", 0)]
    for x in range(1, N_PASS - 2):
        items.append(("w", x))
        items.append(pieces[x - 1])
    items.extend([pieces[N_PASS - 3], ("w", N_PASS - 2), pieces[N_PASS - 2], pieces[N_PASS - 1], ("w", N_PASS - 1)])
    items.extend(pieces[N_PASS:])
    return items


def tile_attention_pa_k_kernel(tc, y_attn, w_proj, b_proj, grad_out, out):
    nc = tc.nc

    g_rows = grad_out.rearrange("(p b) i k -> p (b i) k", b=2)
    w_rows = w_proj.rearrange("(h p e) c -> p h (e c)", p=P, e=2)
    out_rows = out.rearrange("(p b) n (i j) -> p b n i j", b=2, i=2)

    items = stream()
    n_items = len(items)

    with ExitStack() as ctx:
        const = ctx.enter_context(tc.tile_pool(name="const", bufs=1))
        raw_pool = ctx.enter_context(tc.tile_pool(name="raw_pool", bufs=RAW_BUFS))
        grouped_pool = ctx.enter_context(tc.tile_pool(name="grouped_pool", bufs=3))
        g_quantised_pool = ctx.enter_context(tc.tile_pool(name="g_quantised_pool", bufs=8))
        w_quantised_pool = ctx.enter_context(tc.tile_pool(name="w_quantised_pool", bufs=12))
        acc_pool = ctx.enter_context(tc.psum_pool(name="acc_pool", bufs=1))
        bank_pool = ctx.enter_context(tc.psum_pool(name="bank_pool", bufs=4))

        ident = const.tile([P, P], F32, name="ident")
        make_identity(nc, ident[:])
        result = const.tile([P, 2, 2, 2, COLS // 2], F32, name="result")

        acc = [acc_pool.tile([P, COLS], F32, name="acc%d" % m) for m in range(ROW_TILES)]

        raw = {}
        banks = {}
        grouped = {}
        g_quantised = {}
        w_quantised = {}
        enabled = {}
        finished = {}
        done = [0] * ROW_TILES

        def load(n):
            item = items[n]
            if item[0] == "w":
                x = item[1]
                tile = raw_pool.tile([P, PACK * COLS], BF16, name="w_raw")
                nc.sync.dma_start(
                    out=tile[:].rearrange("p (u ec) -> p u ec", u=2),
                    in_=w_rows[:, 2 * x : 2 * x + 2, :],
                )
            else:
                m, x0, passes = item[1:]
                tile = raw_pool.tile([P, passes * K_PASS], BF16, name="g_raw")
                nc.sync.dma_start(out=tile[:], in_=g_rows[:, m, x0 * K_PASS : (x0 + passes) * K_PASS])
            raw[n] = tile

        def transpose_g(n):
            passes = items[n][3]
            words = raw[n][:].bitcast(F32)
            banks[n] = []
            for pair in range(passes // 2):
                bank = bank_pool.tile([P, 2, 2, P], F32, name="bank")
                for aa in range(2):
                    for u in range(2):
                        first = (2 * pair + aa) * WORDS_PASS + u * P
                        nc.tensor.transpose(bank[:, aa, u, :], words[:, first : first + P], ident[:])
                banks[n].append(bank)

        def copy_g(n):
            passes = items[n][3]
            tile = grouped_pool.tile([P, passes * P * PACK], BF16, name="g_grouped", align_bytes=64)
            words = tile[:].bitcast(F32).rearrange("p (a r u) -> p a r u", a=passes, u=2)
            for pair in range(passes // 2):
                nc.scalar.copy(
                    out=words[:, 2 * pair : 2 * pair + 2],
                    in_=banks[n][pair][:].rearrange("p a u r -> p a r u"),
                )
            grouped[n] = tile

        def regroup_w(n):
            tile = grouped_pool.tile([P, COLS * PACK], BF16, name="w_grouped", align_bytes=64)
            dst = tile[:].rearrange("p (c i t) -> p c t i", i=RUN, t=PACK)
            src = raw[n][:].rearrange("p (t c i) -> p c t i", t=PACK, i=RUN)
            split = VECTOR_COLS // RUN
            nc.vector.tensor_copy(out=dst[:, :split], in_=src[:, :split])
            nc.scalar.copy(out=dst[:, split:], in_=src[:, split:])
            grouped[n] = tile

        def quantise(pool, n, width, fp8_x4, name):
            codes = pool.tile([P, width], U32, name=name + "_codes", align_bytes=64)
            scales = pool.tile([P, width], U8, name=name + "_scales", align_bytes=64)
            nc.vector.quantize_mx(out=codes[:].bitcast(fp8_x4), scales=scales[:], in_=grouped[n][:])
            return codes, scales

        def multiply(m, x):
            g_codes, g_scales, first = g_quantised[(m, x)]
            w_codes, w_scales = w_quantised[x]
            g_cols = slice(first, first + P)
            nc.tensor.matmul_mx(
                out=acc[m][:],
                lhsT=g_codes[:, g_cols].bitcast(E5M2_X4),
                lhsT_scale=g_scales[:, g_cols],
                rhs=w_codes[:].bitcast(E4M3_X4),
                rhs_scale=w_scales[:],
                start=(done[m] == 0),
                stop=(done[m] == N_PASS - 1),
            )
            done[m] += 1

        def store(m):
            h, i = divmod(m, 2)
            sums = acc[m][:].rearrange("p (j n) -> p n j", n=2)
            if m < ROW_TILES - 1:
                nc.scalar.copy(out=result[:, h, :, i, :], in_=sums)
                nc.sync.dma_start(out=out_rows[:, h, :, i, :], in_=result[:, h, :, i, :])
            else:
                for n in range(2):
                    nc.vector.tensor_copy(out=result[:, h, n, i, :], in_=sums[:, n, :])
                    nc.sync.dma_start(out=out_rows[:, h, n, i, :], in_=result[:, h, n, i, :])

        def kind(n):
            return items[n][0] if 0 <= n < n_items else ""

        with tc.manual_schedule():
            for tick in range(-LOAD_LEAD, n_items + FLUSH):
                if kind(tick + LOAD_LEAD):
                    load(tick + LOAD_LEAD)
                if kind(tick) == "g" and kind(tick - 1) != "g":
                    n = tick
                    while kind(n) == "g":
                        transpose_g(n)
                        n += 1
                if kind(tick - COPY_LAG) == "g":
                    copy_g(tick - COPY_LAG)
                if kind(tick) == "w":
                    regroup_w(tick)
                new = []
                if kind(tick - G_QUANT_LAG) == "g":
                    n = tick - G_QUANT_LAG
                    m, x0, passes = items[n][1:]
                    codes, scales = quantise(g_quantised_pool, n, passes * P, E5M2_X4, "g")
                    for a in range(passes):
                        g_quantised[(m, x0 + a)] = (codes, scales, a * P)
                        if x0 + a in w_quantised:
                            new.append((m, x0 + a))
                if kind(tick - W_QUANT_LAG) == "w":
                    n = tick - W_QUANT_LAG
                    x = items[n][1]
                    w_quantised[x] = quantise(w_quantised_pool, n, COLS, E4M3_X4, "w")
                    new.extend([(m, x) for m in range(ROW_TILES) if (m, x) in g_quantised])
                enabled[tick] = new
                for m, x in enabled.get(tick - PRODUCT_LAG, []):
                    multiply(m, x)
                    if done[m] == N_PASS:
                        finished[tick] = finished.get(tick, []) + [m]
                for m in finished.get(tick - OUT_LAG, []):
                    store(m)
